import numpy as np
import ml_dtypes


def mxq(x, axis, fmt="e4m3"):
    dtype, down = {"e4m3": (ml_dtypes.float8_e4m3fn, 7), "e5m2": (ml_dtypes.float8_e5m2, 14)}[fmt]
    v = np.moveaxis(np.asarray(x, np.float32).astype(ml_dtypes.bfloat16).astype(np.float64), axis, -1)
    blocks = v.reshape(v.shape[:-1] + (-1, 32))
    amax = np.abs(blocks).max(-1, keepdims=True)
    byte = np.maximum(np.where(amax > 0, np.frexp(amax)[1] - 1 + 127, 0) - down, 1)
    scale = np.exp2(byte - 127.0)
    codes = (blocks / scale).astype(np.float32).astype(dtype).astype(np.float64)
    return np.moveaxis((codes * scale).reshape(v.shape), -1, axis)


WIDE = False


def mx_kscale(k):
    if not WIDE:
        return np.ones(k)
    levels = np.array([30, -30])
    if k % 512:
        return np.exp2(np.random.permutation(np.resize(levels, k // 32))).repeat(32)
    a = np.empty((k // 512, 16))
    for p in range(k // 512):
        a[p, :8] = np.random.permutation(np.resize(levels, 8))
        for g in range(8):
            far = levels[np.abs(levels - a[p, g]) >= 10]
            a[p, g + 8] = far[np.random.randint(len(far))]
    return np.exp2(a.ravel()).repeat(32)


BF16 = ml_dtypes.bfloat16


def bf(x):
    return np.asarray(x, np.float32).astype(BF16)


def f64(x):
    return np.asarray(x).astype(np.float64)


B, T, C, H, NOPE, ROPE, VD, LORA = 1, 512, 2048, 16, 128, 128, 128, 512
QK = NOPE + ROPE
HALF = ROPE // 2


def make_freq_cis():
    inv = 1.0 / (10000.0 ** (np.arange(0, ROPE, 2) / ROPE))
    ang = np.outer(np.arange(T), inv)
    return np.stack([np.cos(ang), np.sin(ang)], -1)


def apply_rope(v, fc):
    vr = v.reshape(B, T, H, HALF, 2)
    f = fc.reshape(1, T, 1, HALF, 2)
    real = vr[..., 0] * f[..., 0] - vr[..., 1] * f[..., 1]
    imag = vr[..., 1] * f[..., 0] + vr[..., 0] * f[..., 1]
    return np.stack([real, imag], -1).reshape(B, T, H, ROPE)


def setup_inputs():
    s = mx_kscale(C)
    return {"x": bf(np.random.standard_normal((B, T, C)) * s),
            "freq_cis": bf(make_freq_cis()),
            "Wq": bf(np.random.standard_normal((C, H * QK)) * 2.0 / np.sqrt(C) / s[:, None])}


def reference(x, freq_cis, Wq):
    q = (mxq(f64(x), 2, "e5m2") @ mxq(f64(Wq), 0, "e4m3")).reshape(B, T, H, QK)
    q_nope, q_rope = q[..., :NOPE], q[..., NOPE:]
    q_rope = apply_rope(q_rope, f64(freq_cis))
    return np.concatenate([q_nope, q_rope], -1)

@@ -1,0 +1,321 @@
+from contextlib import ExitStack
+
+import concourse.mybir as mybir
+from concourse.masks import make_identity
+
+F32 = mybir.dt.float32
+BF16 = mybir.dt.bfloat16
+U32 = mybir.dt.uint32
+U8 = mybir.dt.uint8
+E4M3 = mybir.dt.float8_e4m3fn_x4
+E5M2 = mybir.dt.float8_e5m2_x4
+MULT = mybir.AluOpType.mult
+ADD = mybir.AluOpType.add
+
+TOKENS, K, FEATURES = 512, 2048, 4096
+FLOPS = 2 * TOKENS * K * FEATURES
+
+P = 128
+PACK = 4
+K_PASS = P * PACK
+PASSES = K // K_PASS
+TOK_TILES = TOKENS // P
+N_TILE = 512
+HALF = 128
+CHUNK_HEADS = 4
+CHUNK = CHUNK_HEADS * 2 * HALF
+CHUNKS = FEATURES // CHUNK
+TILES = 2 * CHUNKS
+UNITS = TILES * PASSES
+
+FS = 84
+FS_TAIL = 128
+TAIL_UNITS = 4
+PE_EVEN = 0
+PE_ODD = 0
+RAW_BUFS = 10
+WG_BUFS = 6
+WC_BUFS = 10
+ACC_BUFS = 8
+PROD_BUFS = 5
+STAGE_BUFS = 6
+IL_LEAD = 3
+SUM_LAG = 4
+ALT0 = 1
+UNSKEW_LAST = 1
+FAST_IL = 0
+GSUM = 0
+HEAD_SPLIT = 1
+XORDER = 0
+TAIL_V_KEPT = 0
+X_STEP = 1
+AUX_BUFS = 2
+TAIL_STEP = 28
+
+
+def tile_multiheadlatentattention_pb_kernel(tc, x, freq_cis, Wq, out):
+    nc = tc.nc
+    x2 = x.flatten_outer_dims()
+    out2 = out.rearrange("b t h d -> (b t) (h d)")
+
+    order = []
+    if ALT0:
+        for g in range(PASSES):
+            order.extend([(0, g), (1, g)])
+    else:
+        order.extend([(t, g) for t in range(2) for g in range(PASSES)])
+    order.extend([(t, g) for t in range(2, TILES) for g in range(PASSES)])
+    made = dict((unit, pos) for pos, unit in enumerate(order))
+
+    with ExitStack() as ctx:
+        const = ctx.enter_context(tc.tile_pool(name="const", bufs=1))
+        rawp = ctx.enter_context(tc.tile_pool(name="rawp", bufs=RAW_BUFS))
+        work = ctx.enter_context(tc.tile_pool(name="work", bufs=2))
+        psum = ctx.enter_context(tc.psum_pool(name="psum", bufs=ACC_BUFS))
+
+        ident = const.tile([P, P], F32, name="ident")
+        make_identity(nc, ident[:])
+        if PE_EVEN or PE_ODD:
+            ident_bf = const.tile([P, P], BF16, name="ident_bf")
+            make_identity(nc, ident_bf[:])
+        warm = const.tile([P, 1], F32, name="warm")
+        fc = const.tile([P, TOK_TILES, HALF], BF16, name="fc")
+        tab = const.tile([P, TOK_TILES, 2, HALF], F32, name="tab")
+
+        ctx.enter_context(tc.manual_schedule())
+        nc.scalar.copy(out=warm[:], in_=ident[:, 0:1])
+
+        raw, xraw, xg, xc, xs, xbank = {}, {}, {}, {}, {}, {}
+        wg, wc, ws, acc, prod, stage, aux = {}, {}, {}, {}, {}, {}, {}
+
+        def load_w(i, cuts=(0, CHUNK)):
+            c, g = divmod(i, PASSES)
+            t = rawp.tile([P, PACK, CHUNK], BF16, tag="raw", name="raw%d_%d" % (c, g))
+            rows = Wq[g * K_PASS:(g + 1) * K_PASS, c * CHUNK:(c + 1) * CHUNK].rearrange("(p j) n -> p j n", j=PACK)
+            for lo, hi in zip(cuts[:-1], cuts[1:]):
+                nc.sync.dma_start(out=t[:, :, lo:hi], in_=rows[:, :, lo:hi])
+            raw[(c, g)] = t
+
+        def load_x(a):
+            t = const.tile([P, K], BF16, name="xraw%d" % a)
+            nc.sync.dma_start(out=t[:], in_=x2[a * P:(a + 1) * P, :])
+            xraw[a] = t
+
+        def load_fc():
+            nc.sync.dma_start(out=fc[:], in_=freq_cis.rearrange("(a p) i e -> p a (i e)", p=P))
+
+        load_w(0, (0, 256, 512, 1024) if HEAD_SPLIT else (0, CHUNK))
+        if XORDER == 0:
+            load_x(0); load_x(1); load_w(1); load_x(2); load_x(3); load_fc(); load_w(2); load_w(3)
+        elif XORDER == 1:
+            load_x(0); load_w(1); load_x(1); load_x(2); load_w(2); load_x(3); load_fc(); load_w(3)
+        elif XORDER == 2:
+            load_w(1); load_x(0); load_x(1); load_x(2); load_x(3); load_w(2); load_fc(); load_w(3)
+        for i in range(PASSES, RAW_BUFS):
+            load_w(i)
+
+        fcv = fc[:].rearrange("p a (i e) -> p a i e", e=2)
+        tabv = tab[:].rearrange("p a w (i e) -> p a w i e", e=2)
+        for e in range(2):
+            nc.gpsimd.tensor_copy(out=tabv[:, :, 0, :, e], in_=fcv[:, :, :, 0])
+        nc.gpsimd.tensor_copy(out=tabv[:, :, 1, :, 0], in_=fcv[:, :, :, 1])
+        nc.gpsimd.tensor_scalar(out=tabv[:, :, 1, :, 1], in0=fcv[:, :, :, 1], scalar1=-1.0, scalar2=0.0, op0=MULT, op1=ADD)
+
+        def x_transposes(a):
+            words = xraw[a][:].bitcast(F32)
+            for gp in range(2):
+                bank = psum.tile([P, 2, 2, P], F32, tag="acc", name="xb%d_%d" % (a, gp))
+                for g2 in range(2):
+                    g = 2 * gp + g2
+                    for u in range(2):
+                        nc.tensor.transpose(bank[:, g2, u, :], words[:, 256 * g + u:256 * (g + 1):2], ident[:])
+                xbank[(a, gp)] = bank
+
+        def x_copies(a):
+            t = const.tile([P, PACK * TOKENS], BF16, name="xg%d" % a, align_bytes=64)
+            xg[a] = t
+            tw = t[:].bitcast(F32).rearrange("p (g r u) -> p g r u", g=PASSES, u=2)
+            nc.vector.tensor_copy(out=tw[:, 0:2], in_=xbank[(a, 0)][:].rearrange("p g u r -> p g r u"))
+            nc.scalar.copy(out=tw[:, 2:4], in_=xbank[(a, 1)][:].rearrange("p g u r -> p g r u"))
+
+        def x_quantize(a):
+            xc[a] = const.tile([P, TOKENS], U32, name="xc%d" % a, align_bytes=64)
+            xs[a] = const.tile([P, TOKENS], U8, name="xs%d" % a, align_bytes=64)
+            nc.vector.quantize_mx(out=xc[a][:].bitcast(E5M2), scales=xs[a][:], in_=xg[a][:])
+
+        def pe_heads(pos):
+            return PE_ODD if pos % 2 else PE_EVEN
+
+        def views(pos):
+            tile_i, g = order[pos]
+            c, kept = divmod(tile_i, 2)
+            if pos not in wg:
+                wg[pos] = work.tile([P, PACK * N_TILE], BF16, tag="wg", name="wg%d" % pos, bufs=WG_BUFS, align_bytes=64)
+            src = raw[(c, g)][:].rearrange("p j (h k f) -> p k h f j", k=2, f=HALF)[:, 1 - kept]
+            dst = wg[pos][:].rearrange("p (h f j) -> p h f j", h=CHUNK_HEADS, j=PACK)
+            return src, dst
+
+        def pe_interleave(pos):
+            n = pe_heads(pos)
+            if n == 0:
+                return
+            src, dst = views(pos)
+            t = psum.tile([P, 2 * N_TILE], BF16, tag="aux", name="aux%d" % pos, bufs=AUX_BUFS)
+            aux[pos] = t
+            for i in range(n):
+                nc.tensor.matmul(
+                    out=t[:, i * N_TILE:(i + 1) * N_TILE].rearrange("p (f j) -> p f j", j=PACK),
+                    lhsT=ident_bf[:], rhs=src[:, CHUNK_HEADS - n + i], start=True, stop=True)
+
+        def copy_il(eng_copy, dst, src):
+            if FAST_IL:
+                eng_copy(out=dst.rearrange("p h (b i) j -> p h b j i", i=4), in_=src.rearrange("p h (b i) j -> p h b j i", i=4))
+            else:
+                eng_copy(out=dst, in_=src)
+
+        def interleave(pos, h0=0, h1=CHUNK_HEADS):
+            src, dst = views(pos)
+            n = pe_heads(pos)
+            h1_in = h1
+            h1 = min(h1, CHUNK_HEADS - n)
+            fs = FS_TAIL if pos >= UNITS - TAIL_UNITS else FS
+            if h0 < h1:
+                copy_il(nc.scalar.copy, dst[:, h0:h1, :fs, :], src[:, h0:h1, :fs, :])
+            if n and h1_in == CHUNK_HEADS:
+                nc.scalar.copy(out=wg[pos][:, (CHUNK_HEADS - n) * N_TILE:], in_=aux[pos][:, :n * N_TILE])
+            if fs < HALF and h0 < h1:
+                copy_il(nc.vector.tensor_copy, dst[:, h0:h1, fs:, :], src[:, h0:h1, fs:, :])
+
+        def refill(pos):
+            tile_i, g = order[pos]
+            c, kept = divmod(tile_i, 2)
+            i = c * PASSES + g + RAW_BUFS
+            if kept and i < CHUNKS * PASSES:
+                load_w(i)
+
+        def quantize(pos):
+            wc[pos] = work.tile([P, N_TILE], U32, tag="wc", name="wc%d" % pos, bufs=WC_BUFS, align_bytes=64)
+            ws[pos] = work.tile([P, N_TILE], U8, tag="ws", name="ws%d" % pos, bufs=WC_BUFS, align_bytes=64)
+            nc.vector.quantize_mx(out=wc[pos][:].bitcast(E4M3), scales=ws[pos][:], in_=wg[pos][:])
+
+        def mx_pass(tile_i, a, g):
+            if g == 0:
+                acc[(tile_i, a)] = psum.tile([P, N_TILE], F32, tag="acc", name="acc%d_%d" % (tile_i, a))
+            pos = made[(tile_i, g)]
+            nc.tensor.matmul_mx(
+                out=acc[(tile_i, a)][:],
+                lhsT=xc[a][:, g * P:(g + 1) * P].bitcast(E5M2),
+                lhsT_scale=xs[a][:, g * P:(g + 1) * P],
+                rhs=wc[pos][:].bitcast(E4M3),
+                rhs_scale=ws[pos][:],
+                start=(g == 0),
+                stop=(g == PASSES - 1),
+            )
+
+        def get_stage(c, a):
+            if (c, a) not in stage:
+                stage[(c, a)] = work.tile([P, CHUNK], F32, tag="stage", name="st%d_%d" % (c, a), bufs=STAGE_BUFS)
+            return stage[(c, a)][:].rearrange("p (h k f) -> p h k f", k=2, f=HALF)
+
+        def rope_products(tile_i, a):
+            t = work.tile([P, 2, N_TILE], F32, tag="prod", name="pr%d_%d" % (tile_i, a), bufs=PROD_BUFS)
+            prod[(tile_i, a)] = t
+            shape = [P, 2, CHUNK_HEADS, HALF]
+            nc.vector.tensor_tensor(
+                out=t[:].rearrange("p w (h f) -> p w h f", f=HALF),
+                in0=acc[(tile_i, a)][:].rearrange("p (h f) -> p h f", f=HALF).unsqueeze(1).to_broadcast(shape),
+                in1=tab[:, a].unsqueeze(2).to_broadcast(shape),
+                op=MULT,
+            )
+
+        done = {}
+
+        def finish(c, a):
+            done[(c, a)] = done.get((c, a), 0) + 1
+            if done[(c, a)] == 2:
+                nc.sync.dma_start(out=out2[a * P:(a + 1) * P, c * CHUNK:(c + 1) * CHUNK], in_=stage[(c, a)][:])
+
+        def rope_sum(tile_i, a):
+            t = prod[(tile_i, a)]
+            eng = nc.gpsimd if GSUM else nc.vector
+            eng.tensor_tensor(
+                out=get_stage(tile_i // 2, a)[:, :, 1, :].rearrange("p h (i e) -> p h i e", e=2),
+                in0=t[:, 0].rearrange("p (h i e) -> p h i e", h=CHUNK_HEADS, e=2),
+                in1=t[:, 1].rearrange("p (h i e) -> p h i e", h=CHUNK_HEADS, e=2)[:, :, :, ::-1],
+                op=ADD,
+            )
+            finish(tile_i // 2, a)
+
+        def kept_copy(tile_i, a, on_vector=False):
+            eng_copy = nc.vector.tensor_copy if on_vector else nc.scalar.copy
+            eng_copy(
+                out=get_stage(tile_i // 2, a)[:, :, 0, :],
+                in_=acc[(tile_i, a)][:].rearrange("p (h f) -> p h f", f=HALF),
+            )
+            finish(tile_i // 2, a)
+
+        passes_at, rope_at, kept_at, sum_at = {}, {}, {}, {}
+        x_tr_at = {-2: (0, 1), 0: (2, 3)}
+        x_cp_at = {-1: (0, 1), 0: (2, 3)}
+        x_q_at = {0: (0, 1), 1: (2, 3)}
+        freed = [-1, -1, -1, -1, 0, 0, 0, 0]
+        last_ep = {0: -9, 1: -9}
+        last_sum = -9
+        opened = X_STEP
+        for tile_i in range(TILES):
+            for a in range(TOK_TILES):
+                skew = 0 if tile_i >= TILES - UNSKEW_LAST else a
+                st = max(tile_i * PASSES + skew, freed[len(freed) - ACC_BUFS] + 1, opened)
+                opened = st
+                for g in range(PASSES):
+                    st = max(st + (1 if g else 0), made[(tile_i, g)])
+                    passes_at.setdefault(st, []).append((tile_i, a, g))
+                kept = tile_i % 2
+                ep = max(st + 1, last_ep[kept] + 1)
+                if tile_i == TILES - 1:
+                    ep = st + 1
+                last_ep[kept] = ep
+                freed.append(ep)
+                (kept_at if kept else rope_at).setdefault(ep, []).append((tile_i, a))
+                if not kept:
+                    last_sum = max(ep + (SUM_LAG if tile_i < TILES - 2 else 1), last_sum + 1)
+                    sum_at.setdefault(last_sum, []).append((tile_i, a))
+        n_steps = max(max(kept_at), max(sum_at)) + 1
+
+        def step(s):
+            if 0 <= s + 1 < UNITS:
+                quantize(s + 1)
+            for a in x_q_at.get(s, ()):
+                x_quantize(a)
+            for a in x_tr_at.get(s, ()):
+                x_transposes(a)
+            for (tile_i, a, g) in passes_at.get(s, []):
+                mx_pass(tile_i, a, g)
+            for (tile_i, a) in rope_at.get(s, []):
+                rope_products(tile_i, a)
+            for i, (tile_i, a) in enumerate(kept_at.get(s, [])):
+                kept_copy(tile_i, a, on_vector=(TAIL_V_KEPT and i % 2 == 1))
+            for (tile_i, a) in sum_at.get(s, []):
+                rope_sum(tile_i, a)
+            if s == -1:
+                for a in x_cp_at.get(s, ()):
+                    x_copies(a)
+            pos = s + IL_LEAD
+            if s == -IL_LEAD:
+                for h0, h1 in (((0, 1), (1, 2), (2, 4)) if HEAD_SPLIT else ((0, 4),)):
+                    interleave(0, h0, h1)
+                    interleave(1, h0, h1)
+                refill(1)
+            elif 2 <= pos < UNITS:
+                interleave(pos)
+                refill(pos)
+            if s != -1:
+                for a in x_cp_at.get(s, ()):
+                    x_copies(a)
+            if 2 <= pos + 1 < UNITS:
+                pe_interleave(pos + 1)
+
+        pe_interleave(0)
+        pe_interleave(1)
+        for s in range(-IL_LEAD, n_steps):
+            step(s)

@@ -28,15 +28,15 @@ CHUNKS = FEATURES // CHUNK
 TILES = 2 * CHUNKS
 UNITS = TILES * PASSES
 
-FS = 84
+FS = 80
 FS_TAIL = 128
 TAIL_UNITS = 4
-PE_EVEN = 0
-PE_ODD = 0
+PE_EVEN = 1
+PE_ODD = 2
 RAW_BUFS = 10
 WG_BUFS = 6
 WC_BUFS = 10
-ACC_BUFS = 8
+ACC_BUFS = 6
 PROD_BUFS = 5
 STAGE_BUFS = 6
 IL_LEAD = 3

@@ -28,29 +28,22 @@ CHUNKS = FEATURES // CHUNK
 TILES = 2 * CHUNKS
 UNITS = TILES * PASSES
 
-FS = 80
-FS_TAIL = 128
-TAIL_UNITS = 4
-PE_EVEN = 1
-PE_ODD = 2
+V_UNITS = (1, 4, 7, 10, 13, 15, 18, 21, 23, 26)
+SPLIT = dict((pos, 128 if pos >= 28 else 84) for pos in range(32))
 RAW_BUFS = 10
 WG_BUFS = 6
 WC_BUFS = 10
-ACC_BUFS = 6
+ACC_BUFS = 8
 PROD_BUFS = 5
 STAGE_BUFS = 6
 IL_LEAD = 3
 SUM_LAG = 4
-ALT0 = 1
 UNSKEW_LAST = 1
-FAST_IL = 0
-GSUM = 0
-HEAD_SPLIT = 1
-XORDER = 0
-TAIL_V_KEPT = 0
-X_STEP = 1
-AUX_BUFS = 2
-TAIL_STEP = 28
+FAST_IL = 1
+X0 = 1
+TAB_STEP = 5
+W_FIRST = 3
+QW = 1
 
 
 def tile_multiheadlatentattention_pb_kernel(tc, x, freq_cis, Wq, out):
@@ -59,13 +52,39 @@ def tile_multiheadlatentattention_pb_kernel(tc, x, freq_cis, Wq, out):
     out2 = out.rearrange("b t h d -> (b t) (h d)")
 
     order = []
-    if ALT0:
-        for g in range(PASSES):
-            order.extend([(0, g), (1, g)])
-    else:
-        order.extend([(t, g) for t in range(2) for g in range(PASSES)])
+    for g in range(PASSES):
+        order.extend([(0, g), (1, g)])
     order.extend([(t, g) for t in range(2, TILES) for g in range(PASSES)])
-    made = dict((unit, pos) for pos, unit in enumerate(order))
+    place = dict((unit, pos) for pos, unit in enumerate(order))
+    made = dict((unit, QW * (pos // QW) + QW - 1) for pos, unit in enumerate(order))
+
+    passes_at, rope_at, kept_at, sum_at = {}, {}, {}, {}
+    x_tr_at = {X0: (0, 1), X0 + 1: (2, 3)}
+    x_cp_at = {X0 + 1: (0, 1), X0 + 2: (2, 3)}
+    x_q_at = {X0 + 2: (0, 1), X0 + 3: (2, 3)}
+    freed = [X0 + 1] * 4 + [X0 + 2] * 4
+    last_ep = {0: -9, 1: -9}
+    last_sum = -9
+    opened = X0 + 3
+    for tile_i in range(TILES):
+        for a in range(TOK_TILES):
+            skew = 0 if tile_i >= TILES - UNSKEW_LAST else a
+            st = max(tile_i * PASSES + skew, freed[len(freed) - ACC_BUFS] + 1, opened)
+            opened = st
+            for g in range(PASSES):
+                st = max(st + (1 if g else 0), made[(tile_i, g)])
+                passes_at.setdefault(st, []).append((tile_i, a, g))
+            kept = tile_i % 2
+            ep = max(st + 1, last_ep[kept] + 1)
+            if tile_i == TILES - 1:
+                ep = st + 1
+            last_ep[kept] = ep
+            freed.append(ep)
+            (kept_at if kept else rope_at).setdefault(ep, []).append((tile_i, a))
+            if not kept:
+                last_sum = max(ep + (SUM_LAG if tile_i < TILES - 2 else 1), last_sum + 1)
+                sum_at.setdefault(last_sum, []).append((tile_i, a))
+    n_steps = max(max(kept_at), max(sum_at)) + 1
 
     with ExitStack() as ctx:
         const = ctx.enter_context(tc.tile_pool(name="const", bufs=1))
@@ -75,10 +94,10 @@ def tile_multiheadlatentattention_pb_kernel(tc, x, freq_cis, Wq, out):
 
         ident = const.tile([P, P], F32, name="ident")
         make_identity(nc, ident[:])
-        if PE_EVEN or PE_ODD:
-            ident_bf = const.tile([P, P], BF16, name="ident_bf")
-            make_identity(nc, ident_bf[:])
         warm = const.tile([P, 1], F32, name="warm")
+        sign = const.tile([P, 2], F32, name="sign")
+        nc.gpsimd.memset(sign[:, 0:1], 1.0)
+        nc.gpsimd.memset(sign[:, 1:2], -1.0)
         fc = const.tile([P, TOK_TILES, HALF], BF16, name="fc")
         tab = const.tile([P, TOK_TILES, 2, HALF], F32, name="tab")
 
@@ -86,7 +105,7 @@ def tile_multiheadlatentattention_pb_kernel(tc, x, freq_cis, Wq, out):
         nc.scalar.copy(out=warm[:], in_=ident[:, 0:1])
 
         raw, xraw, xg, xc, xs, xbank = {}, {}, {}, {}, {}, {}
-        wg, wc, ws, acc, prod, stage, aux = {}, {}, {}, {}, {}, {}, {}
+        wg, wc, ws, acc, prod, stage, done = {}, {}, {}, {}, {}, {}, {}
 
         def load_w(i, cuts=(0, CHUNK)):
             c, g = divmod(i, PASSES)
@@ -101,25 +120,23 @@ def tile_multiheadlatentattention_pb_kernel(tc, x, freq_cis, Wq, out):
             nc.sync.dma_start(out=t[:], in_=x2[a * P:(a + 1) * P, :])
             xraw[a] = t
 
-        def load_fc():
-            nc.sync.dma_start(out=fc[:], in_=freq_cis.rearrange("(a p) i e -> p a (i e)", p=P))
-
-        load_w(0, (0, 256, 512, 1024) if HEAD_SPLIT else (0, CHUNK))
-        if XORDER == 0:
-            load_x(0); load_x(1); load_w(1); load_x(2); load_x(3); load_fc(); load_w(2); load_w(3)
-        elif XORDER == 1:
-            load_x(0); load_w(1); load_x(1); load_x(2); load_w(2); load_x(3); load_fc(); load_w(3)
-        elif XORDER == 2:
-            load_w(1); load_x(0); load_x(1); load_x(2); load_x(3); load_w(2); load_fc(); load_w(3)
-        for i in range(PASSES, RAW_BUFS):
+        load_w(0, (0, 256, 512, 1024))
+        for i in range(1, W_FIRST):
+            load_w(i)
+        for a in range(TOK_TILES):
+            load_x(a)
+        nc.sync.dma_start(out=fc[:], in_=freq_cis.rearrange("(a p) i e -> p a (i e)", p=P))
+        for i in range(W_FIRST, RAW_BUFS):
             load_w(i)
 
-        fcv = fc[:].rearrange("p a (i e) -> p a i e", e=2)
-        tabv = tab[:].rearrange("p a w (i e) -> p a w i e", e=2)
-        for e in range(2):
-            nc.gpsimd.tensor_copy(out=tabv[:, :, 0, :, e], in_=fcv[:, :, :, 0])
-        nc.gpsimd.tensor_copy(out=tabv[:, :, 1, :, 0], in_=fcv[:, :, :, 1])
-        nc.gpsimd.tensor_scalar(out=tabv[:, :, 1, :, 1], in0=fcv[:, :, :, 1], scalar1=-1.0, scalar2=0.0, op0=MULT, op1=ADD)
+        def make_tables():
+            fcv = fc[:].rearrange("p a (i e) -> p a i e", e=2)
+            tabv = tab[:].rearrange("p a w (i e) -> p a w i e", e=2)
+            shape = [P, TOK_TILES, HALF // 2, 2]
+            nc.vector.tensor_copy(out=tabv[:, :, 0], in_=fcv[:, :, :, 0:1].to_broadcast(shape))
+            nc.vector.tensor_tensor(
+                out=tabv[:, :, 1], in0=fcv[:, :, :, 1:2].to_broadcast(shape),
+                in1=sign[:].unsqueeze(1).unsqueeze(1).to_broadcast(shape), op=MULT)
 
         def x_transposes(a):
             words = xraw[a][:].bitcast(F32)
@@ -143,30 +160,6 @@ def tile_multiheadlatentattention_pb_kernel(tc, x, freq_cis, Wq, out):
             xs[a] = const.tile([P, TOKENS], U8, name="xs%d" % a, align_bytes=64)
             nc.vector.quantize_mx(out=xc[a][:].bitcast(E5M2), scales=xs[a][:], in_=xg[a][:])
 
-        def pe_heads(pos):
-            return PE_ODD if pos % 2 else PE_EVEN
-
-        def views(pos):
-            tile_i, g = order[pos]
-            c, kept = divmod(tile_i, 2)
-            if pos not in wg:
-                wg[pos] = work.tile([P, PACK * N_TILE], BF16, tag="wg", name="wg%d" % pos, bufs=WG_BUFS, align_bytes=64)
-            src = raw[(c, g)][:].rearrange("p j (h k f) -> p k h f j", k=2, f=HALF)[:, 1 - kept]
-            dst = wg[pos][:].rearrange("p (h f j) -> p h f j", h=CHUNK_HEADS, j=PACK)
-            return src, dst
-
-        def pe_interleave(pos):
-            n = pe_heads(pos)
-            if n == 0:
-                return
-            src, dst = views(pos)
-            t = psum.tile([P, 2 * N_TILE], BF16, tag="aux", name="aux%d" % pos, bufs=AUX_BUFS)
-            aux[pos] = t
-            for i in range(n):
-                nc.tensor.matmul(
-                    out=t[:, i * N_TILE:(i + 1) * N_TILE].rearrange("p (f j) -> p f j", j=PACK),
-                    lhsT=ident_bf[:], rhs=src[:, CHUNK_HEADS - n + i], start=True, stop=True)
-
         def copy_il(eng_copy, dst, src):
             if FAST_IL:
                 eng_copy(out=dst.rearrange("p h (b i) j -> p h b j i", i=4), in_=src.rearrange("p h (b i) j -> p h b j i", i=4))
@@ -174,16 +167,17 @@ def tile_multiheadlatentattention_pb_kernel(tc, x, freq_cis, Wq, out):
                 eng_copy(out=dst, in_=src)
 
         def interleave(pos, h0=0, h1=CHUNK_HEADS):
-            src, dst = views(pos)
-            n = pe_heads(pos)
-            h1_in = h1
-            h1 = min(h1, CHUNK_HEADS - n)
-            fs = FS_TAIL if pos >= UNITS - TAIL_UNITS else FS
-            if h0 < h1:
+            tile_i, g = order[pos]
+            c, kept = divmod(tile_i, 2)
+            m, half = divmod(pos, QW)
+            if m not in wg:
+                wg[m] = work.tile([P, QW, PACK * N_TILE], BF16, tag="wg", name="wg%d" % m, bufs=WG_BUFS, align_bytes=64)
+            src = raw[(c, g)][:].rearrange("p j (h k f) -> p k h f j", k=2, f=HALF)[:, 1 - kept]
+            dst = wg[m][:, half].rearrange("p (h f j) -> p h f j", h=CHUNK_HEADS, j=PACK)
+            fs = SPLIT.get(pos, 0 if pos in V_UNITS else HALF)
+            if fs > 0:
                 copy_il(nc.scalar.copy, dst[:, h0:h1, :fs, :], src[:, h0:h1, :fs, :])
-            if n and h1_in == CHUNK_HEADS:
-                nc.scalar.copy(out=wg[pos][:, (CHUNK_HEADS - n) * N_TILE:], in_=aux[pos][:, :n * N_TILE])
-            if fs < HALF and h0 < h1:
+            if fs < HALF:
                 copy_il(nc.vector.tensor_copy, dst[:, h0:h1, fs:, :], src[:, h0:h1, fs:, :])
 
         def refill(pos):
@@ -193,21 +187,22 @@ def tile_multiheadlatentattention_pb_kernel(tc, x, freq_cis, Wq, out):
             if kept and i < CHUNKS * PASSES:
                 load_w(i)
 
-        def quantize(pos):
-            wc[pos] = work.tile([P, N_TILE], U32, tag="wc", name="wc%d" % pos, bufs=WC_BUFS, align_bytes=64)
-            ws[pos] = work.tile([P, N_TILE], U8, tag="ws", name="ws%d" % pos, bufs=WC_BUFS, align_bytes=64)
-            nc.vector.quantize_mx(out=wc[pos][:].bitcast(E4M3), scales=ws[pos][:], in_=wg[pos][:])
+        def quantize(m):
+            wc[m] = work.tile([P, QW * N_TILE], U32, tag="wc", name="wc%d" % m, bufs=WC_BUFS, align_bytes=64)
+            ws[m] = work.tile([P, QW * N_TILE], U8, tag="ws", name="ws%d" % m, bufs=WC_BUFS, align_bytes=64)
+            nc.vector.quantize_mx(out=wc[m][:].bitcast(E4M3), scales=ws[m][:], in_=wg[m][:].rearrange("p q n -> p (q n)"))
 
         def mx_pass(tile_i, a, g):
             if g == 0:
                 acc[(tile_i, a)] = psum.tile([P, N_TILE], F32, tag="acc", name="acc%d_%d" % (tile_i, a))
-            pos = made[(tile_i, g)]
+            m, half = divmod(place[(tile_i, g)], QW)
+            cols = slice(half * N_TILE, (half + 1) * N_TILE)
             nc.tensor.matmul_mx(
                 out=acc[(tile_i, a)][:],
                 lhsT=xc[a][:, g * P:(g + 1) * P].bitcast(E5M2),
                 lhsT_scale=xs[a][:, g * P:(g + 1) * P],
-                rhs=wc[pos][:].bitcast(E4M3),
-                rhs_scale=ws[pos][:],
+                rhs=wc[m][:, cols].bitcast(E4M3),
+                rhs_scale=ws[m][:, cols],
                 start=(g == 0),
                 stop=(g == PASSES - 1),
             )
@@ -216,6 +211,11 @@ def tile_multiheadlatentattention_pb_kernel(tc, x, freq_cis, Wq, out):
             if (c, a) not in stage:
                 stage[(c, a)] = work.tile([P, CHUNK], F32, tag="stage", name="st%d_%d" % (c, a), bufs=STAGE_BUFS)
             return stage[(c, a)][:].rearrange("p (h k f) -> p h k f", k=2, f=HALF)
+
+        def finish(c, a):
+            done[(c, a)] = done.get((c, a), 0) + 1
+            if done[(c, a)] == 2:
+                nc.sync.dma_start(out=out2[a * P:(a + 1) * P, c * CHUNK:(c + 1) * CHUNK], in_=stage[(c, a)][:])
 
         def rope_products(tile_i, a):
             t = work.tile([P, 2, N_TILE], F32, tag="prod", name="pr%d_%d" % (tile_i, a), bufs=PROD_BUFS)
@@ -228,17 +228,9 @@ def tile_multiheadlatentattention_pb_kernel(tc, x, freq_cis, Wq, out):
                 op=MULT,
             )
 
-        done = {}
-
-        def finish(c, a):
-            done[(c, a)] = done.get((c, a), 0) + 1
-            if done[(c, a)] == 2:
-                nc.sync.dma_start(out=out2[a * P:(a + 1) * P, c * CHUNK:(c + 1) * CHUNK], in_=stage[(c, a)][:])
-
         def rope_sum(tile_i, a):
             t = prod[(tile_i, a)]
-            eng = nc.gpsimd if GSUM else nc.vector
-            eng.tensor_tensor(
+            nc.vector.tensor_tensor(
                 out=get_stage(tile_i // 2, a)[:, :, 1, :].rearrange("p h (i e) -> p h i e", e=2),
                 in0=t[:, 0].rearrange("p (h i e) -> p h i e", h=CHUNK_HEADS, e=2),
                 in1=t[:, 1].rearrange("p (h i e) -> p h i e", h=CHUNK_HEADS, e=2)[:, :, :, ::-1],
@@ -246,76 +238,41 @@ def tile_multiheadlatentattention_pb_kernel(tc, x, freq_cis, Wq, out):
             )
             finish(tile_i // 2, a)
 
-        def kept_copy(tile_i, a, on_vector=False):
-            eng_copy = nc.vector.tensor_copy if on_vector else nc.scalar.copy
-            eng_copy(
+        def kept_copy(tile_i, a):
+            nc.scalar.copy(
                 out=get_stage(tile_i // 2, a)[:, :, 0, :],
                 in_=acc[(tile_i, a)][:].rearrange("p (h f) -> p h f", f=HALF),
             )
             finish(tile_i // 2, a)
 
-        passes_at, rope_at, kept_at, sum_at = {}, {}, {}, {}
-        x_tr_at = {-2: (0, 1), 0: (2, 3)}
-        x_cp_at = {-1: (0, 1), 0: (2, 3)}
-        x_q_at = {0: (0, 1), 1: (2, 3)}
-        freed = [-1, -1, -1, -1, 0, 0, 0, 0]
-        last_ep = {0: -9, 1: -9}
-        last_sum = -9
-        opened = X_STEP
-        for tile_i in range(TILES):
-            for a in range(TOK_TILES):
-                skew = 0 if tile_i >= TILES - UNSKEW_LAST else a
-                st = max(tile_i * PASSES + skew, freed[len(freed) - ACC_BUFS] + 1, opened)
-                opened = st
-                for g in range(PASSES):
-                    st = max(st + (1 if g else 0), made[(tile_i, g)])
-                    passes_at.setdefault(st, []).append((tile_i, a, g))
-                kept = tile_i % 2
-                ep = max(st + 1, last_ep[kept] + 1)
-                if tile_i == TILES - 1:
-                    ep = st + 1
-                last_ep[kept] = ep
-                freed.append(ep)
-                (kept_at if kept else rope_at).setdefault(ep, []).append((tile_i, a))
-                if not kept:
-                    last_sum = max(ep + (SUM_LAG if tile_i < TILES - 2 else 1), last_sum + 1)
-                    sum_at.setdefault(last_sum, []).append((tile_i, a))
-        n_steps = max(max(kept_at), max(sum_at)) + 1
-
         def step(s):
-            if 0 <= s + 1 < UNITS:
-                quantize(s + 1)
+            if 0 <= s + 1 < UNITS and (s + 1) % QW == QW - 1:
+                quantize((s + 1) // QW)
             for a in x_q_at.get(s, ()):
                 x_quantize(a)
+            if s == TAB_STEP:
+                make_tables()
             for a in x_tr_at.get(s, ()):
                 x_transposes(a)
             for (tile_i, a, g) in passes_at.get(s, []):
                 mx_pass(tile_i, a, g)
             for (tile_i, a) in rope_at.get(s, []):
                 rope_products(tile_i, a)
-            for i, (tile_i, a) in enumerate(kept_at.get(s, [])):
-                kept_copy(tile_i, a, on_vector=(TAIL_V_KEPT and i % 2 == 1))
+            for (tile_i, a) in kept_at.get(s, []):
+                kept_copy(tile_i, a)
             for (tile_i, a) in sum_at.get(s, []):
                 rope_sum(tile_i, a)
-            if s == -1:
-                for a in x_cp_at.get(s, ()):
-                    x_copies(a)
+            for a in x_cp_at.get(s, ()):
+                x_copies(a)
             pos = s + IL_LEAD
             if s == -IL_LEAD:
-                for h0, h1 in (((0, 1), (1, 2), (2, 4)) if HEAD_SPLIT else ((0, 4),)):
+                for h0, h1 in ((0, 1), (1, 2), (2, 4)):
                     interleave(0, h0, h1)
                     interleave(1, h0, h1)
                 refill(1)
             elif 2 <= pos < UNITS:
                 interleave(pos)
                 refill(pos)
-            if s != -1:
-                for a in x_cp_at.get(s, ()):
-                    x_copies(a)
-            if 2 <= pos + 1 < UNITS:
-                pe_interleave(pos + 1)
 
-        pe_interleave(0)
-        pe_interleave(1)
         for s in range(-IL_LEAD, n_steps):
             step(s)

@@ -29,7 +29,8 @@ TILES = 2 * CHUNKS
 UNITS = TILES * PASSES
 
 V_UNITS = (1, 4, 7, 10, 13, 15, 18, 21, 23, 26)
-SPLIT = dict((pos, 128 if pos >= 28 else 84) for pos in range(32))
+SPLIT = dict((pos, 128 if pos >= 28 else 72) for pos in range(32))
+G_HELP = 1
 RAW_BUFS = 10
 WG_BUFS = 6
 WC_BUFS = 10
@@ -161,7 +162,9 @@ def tile_multiheadlatentattention_pb_kernel(tc, x, freq_cis, Wq, out):
             nc.vector.quantize_mx(out=xc[a][:].bitcast(E5M2), scales=xs[a][:], in_=xg[a][:])
 
         def copy_il(eng_copy, dst, src):
-            if FAST_IL:
+            if dst.shape[1] == 1:
+                eng_copy(out=dst[:, 0].rearrange("p (b i) j -> p b j i", i=4), in_=src[:, 0].rearrange("p (b i) j -> p b j i", i=4))
+            elif FAST_IL:
                 eng_copy(out=dst.rearrange("p h (b i) j -> p h b j i", i=4), in_=src.rearrange("p h (b i) j -> p h b j i", i=4))
             else:
                 eng_copy(out=dst, in_=src)
@@ -174,6 +177,11 @@ def tile_multiheadlatentattention_pb_kernel(tc, x, freq_cis, Wq, out):
                 wg[m] = work.tile([P, QW, PACK * N_TILE], BF16, tag="wg", name="wg%d" % m, bufs=WG_BUFS, align_bytes=64)
             src = raw[(c, g)][:].rearrange("p j (h k f) -> p k h f j", k=2, f=HALF)[:, 1 - kept]
             dst = wg[m][:, half].rearrange("p (h f j) -> p h f j", h=CHUNK_HEADS, j=PACK)
+            if G_HELP and (pos - WG_BUFS - 1) in rope_at:
+                hg = CHUNK_HEADS - 1
+                copy_il(nc.scalar.copy, dst[:, :hg], src[:, :hg])
+                nc.gpsimd.tensor_scalar(out=dst[:, hg], in0=src[:, hg], scalar1=1.0, scalar2=0.0, op0=MULT, op1=ADD)
+                return
             fs = SPLIT.get(pos, 0 if pos in V_UNITS else HALF)
             if fs > 0:
                 copy_il(nc.scalar.copy, dst[:, h0:h1, :fs, :], src[:, h0:h1, :fs, :])

@@ -31,12 +31,13 @@ UNITS = TILES * PASSES
 V_UNITS = (1, 4, 7, 10, 13, 15, 18, 21, 23, 26)
 SPLIT = dict((pos, 128 if pos >= 28 else 72) for pos in range(32))
 G_HELP = 1
+ALT_CHUNKS = 2
 RAW_BUFS = 10
 WG_BUFS = 6
 WC_BUFS = 10
 ACC_BUFS = 8
 PROD_BUFS = 5
-STAGE_BUFS = 6
+STAGE_BUFS = 8
 IL_LEAD = 3
 SUM_LAG = 4
 UNSKEW_LAST = 1
@@ -53,9 +54,10 @@ def tile_multiheadlatentattention_pb_kernel(tc, x, freq_cis, Wq, out):
     out2 = out.rearrange("b t h d -> (b t) (h d)")
 
     order = []
-    for g in range(PASSES):
-        order.extend([(0, g), (1, g)])
-    order.extend([(t, g) for t in range(2, TILES) for g in range(PASSES)])
+    for c in range(ALT_CHUNKS):
+        for g in range(PASSES):
+            order.extend([(2 * c, g), (2 * c + 1, g)])
+    order.extend([(t, g) for t in range(2 * ALT_CHUNKS, TILES) for g in range(PASSES)])
     place = dict((unit, pos) for pos, unit in enumerate(order))
     made = dict((unit, QW * (pos // QW) + QW - 1) for pos, unit in enumerate(order))
 
@@ -161,9 +163,9 @@ def tile_multiheadlatentattention_pb_kernel(tc, x, freq_cis, Wq, out):
             xs[a] = const.tile([P, TOKENS], U8, name="xs%d" % a, align_bytes=64)
             nc.vector.quantize_mx(out=xc[a][:].bitcast(E5M2), scales=xs[a][:], in_=xg[a][:])
 
-        def copy_il(eng_copy, dst, src):
-            if dst.shape[1] == 1:
-                eng_copy(out=dst[:, 0].rearrange("p (b i) j -> p b j i", i=4), in_=src[:, 0].rearrange("p (b i) j -> p b j i", i=4))
+        def copy_il(eng_copy, dst, src, plain=False):
+            if plain:
+                eng_copy(out=dst, in_=src)
             elif FAST_IL:
                 eng_copy(out=dst.rearrange("p h (b i) j -> p h b j i", i=4), in_=src.rearrange("p h (b i) j -> p h b j i", i=4))
             else:
@@ -184,9 +186,9 @@ def tile_multiheadlatentattention_pb_kernel(tc, x, freq_cis, Wq, out):
                 return
             fs = SPLIT.get(pos, 0 if pos in V_UNITS else HALF)
             if fs > 0:
-                copy_il(nc.scalar.copy, dst[:, h0:h1, :fs, :], src[:, h0:h1, :fs, :])
+                copy_il(nc.scalar.copy, dst[:, h0:h1, :fs, :], src[:, h0:h1, :fs, :], plain=(pos < 2))
             if fs < HALF:
-                copy_il(nc.vector.tensor_copy, dst[:, h0:h1, fs:, :], src[:, h0:h1, fs:, :])
+                copy_il(nc.vector.tensor_copy, dst[:, h0:h1, fs:, :], src[:, h0:h1, fs:, :], plain=(pos < 2))
 
         def refill(pos):
             tile_i, g = order[pos]

@@ -29,7 +29,20 @@ TILES = 2 * CHUNKS
 UNITS = TILES * PASSES
 
 V_UNITS = (1, 4, 7, 10, 13, 15, 18, 21, 23, 26)
-SPLIT = dict((pos, 128 if pos >= 28 else 72) for pos in range(32))
+KLAG = 0
+X_FIRST = 1
+X_COPY_S = 0
+TAB_S = 0
+HEAD_UNITS = 8
+FS_HEAD = 64
+KLAG_TILES = 2
+S_ONLY_FROM = 28
+FS_FREE = 80
+FS_ONE = 80
+FS_BOTH = 80
+SEQ = (0, 1, 2, 3, 4, 5, 6, 7)
+SUM_LAG_END = 1
+END_TILES = 2
 G_HELP = 1
 ALT_CHUNKS = 2
 RAW_BUFS = 10
@@ -37,7 +50,7 @@ WG_BUFS = 6
 WC_BUFS = 10
 ACC_BUFS = 8
 PROD_BUFS = 5
-STAGE_BUFS = 8
+STAGE_BUFS = 12
 IL_LEAD = 3
 SUM_LAG = 4
 UNSKEW_LAST = 1
@@ -57,35 +70,35 @@ def tile_multiheadlatentattention_pb_kernel(tc, x, freq_cis, Wq, out):
     for c in range(ALT_CHUNKS):
         for g in range(PASSES):
             order.extend([(2 * c, g), (2 * c + 1, g)])
-    order.extend([(t, g) for t in range(2 * ALT_CHUNKS, TILES) for g in range(PASSES)])
+    order.extend([(t, g) for t in SEQ[2 * ALT_CHUNKS:] for g in range(PASSES)])
     place = dict((unit, pos) for pos, unit in enumerate(order))
     made = dict((unit, QW * (pos // QW) + QW - 1) for pos, unit in enumerate(order))
 
     passes_at, rope_at, kept_at, sum_at = {}, {}, {}, {}
-    x_tr_at = {X0: (0, 1), X0 + 1: (2, 3)}
-    x_cp_at = {X0 + 1: (0, 1), X0 + 2: (2, 3)}
-    x_q_at = {X0 + 2: (0, 1), X0 + 3: (2, 3)}
-    freed = [X0 + 1] * 4 + [X0 + 2] * 4
+    x_tr_at = {} if X_FIRST else {X0: (0, 1), X0 + 1: (2, 3)}
+    x_cp_at = {} if X_FIRST else {X0 + 1: (0, 1), X0 + 2: (2, 3)}
+    x_q_at = {} if X_FIRST else {X0 + 2: (0, 1), X0 + 3: (2, 3)}
+    freed = [-9] * 8 if X_FIRST else [X0 + 1] * 4 + [X0 + 2] * 4
     last_ep = {0: -9, 1: -9}
     last_sum = -9
-    opened = X0 + 3
-    for tile_i in range(TILES):
+    opened = -1 if X_FIRST else X0 + 3
+    for n, tile_i in enumerate(SEQ):
         for a in range(TOK_TILES):
-            skew = 0 if tile_i >= TILES - UNSKEW_LAST else a
-            st = max(tile_i * PASSES + skew, freed[len(freed) - ACC_BUFS] + 1, opened)
+            skew = 0 if n >= TILES - UNSKEW_LAST else a
+            st = max(n * PASSES + skew, freed[len(freed) - ACC_BUFS] + 1, opened)
             opened = st
             for g in range(PASSES):
                 st = max(st + (1 if g else 0), made[(tile_i, g)])
                 passes_at.setdefault(st, []).append((tile_i, a, g))
             kept = tile_i % 2
-            ep = max(st + 1, last_ep[kept] + 1)
-            if tile_i == TILES - 1:
+            ep = max(st + 1 + (KLAG if kept and n < KLAG_TILES else 0), last_ep[kept] + 1)
+            if n == TILES - 1:
                 ep = st + 1
             last_ep[kept] = ep
             freed.append(ep)
             (kept_at if kept else rope_at).setdefault(ep, []).append((tile_i, a))
             if not kept:
-                last_sum = max(ep + (SUM_LAG if tile_i < TILES - 2 else 1), last_sum + 1)
+                last_sum = max(ep + (SUM_LAG if n < TILES - 1 - END_TILES else SUM_LAG_END), last_sum + 1)
                 sum_at.setdefault(last_sum, []).append((tile_i, a))
     n_steps = max(max(kept_at), max(sum_at)) + 1
 
@@ -119,15 +132,22 @@ def tile_multiheadlatentattention_pb_kernel(tc, x, freq_cis, Wq, out):
             raw[(c, g)] = t
 
         def load_x(a):
-            t = const.tile([P, K], BF16, name="xraw%d" % a)
+            t = work.tile([P, K], BF16, tag="stage", name="xraw%d" % a, bufs=STAGE_BUFS, align_bytes=64)
             nc.sync.dma_start(out=t[:], in_=x2[a * P:(a + 1) * P, :])
             xraw[a] = t
 
-        load_w(0, (0, 256, 512, 1024))
-        for i in range(1, W_FIRST):
-            load_w(i)
-        for a in range(TOK_TILES):
-            load_x(a)
+        if X_FIRST:
+            for a in range(TOK_TILES):
+                load_x(a)
+            load_w(0, (0, 256, 512, 1024))
+            for i in range(1, W_FIRST):
+                load_w(i)
+        else:
+            load_w(0, (0, 256, 512, 1024))
+            for i in range(1, W_FIRST):
+                load_w(i)
+            for a in range(TOK_TILES):
+                load_x(a)
         nc.sync.dma_start(out=fc[:], in_=freq_cis.rearrange("(a p) i e -> p a (i e)", p=P))
         for i in range(W_FIRST, RAW_BUFS):
             load_w(i)
@@ -136,6 +156,11 @@ def tile_multiheadlatentattention_pb_kernel(tc, x, freq_cis, Wq, out):
             fcv = fc[:].rearrange("p a (i e) -> p a i e", e=2)
             tabv = tab[:].rearrange("p a w (i e) -> p a w i e", e=2)
             shape = [P, TOK_TILES, HALF // 2, 2]
+            if TAB_S:
+                nc.scalar.copy(out=tabv[:, :, 0], in_=fcv[:, :, :, 0:1].to_broadcast(shape))
+                nc.scalar.copy(out=tabv[:, :, 1, :, 0:1], in_=fcv[:, :, :, 1:2])
+                nc.scalar.mul(out=tabv[:, :, 1, :, 1:2], in_=fcv[:, :, :, 1:2], mul=-1.0)
+                return
             nc.vector.tensor_copy(out=tabv[:, :, 0], in_=fcv[:, :, :, 0:1].to_broadcast(shape))
             nc.vector.tensor_tensor(
                 out=tabv[:, :, 1], in0=fcv[:, :, :, 1:2].to_broadcast(shape),
@@ -152,10 +177,11 @@ def tile_multiheadlatentattention_pb_kernel(tc, x, freq_cis, Wq, out):
                 xbank[(a, gp)] = bank
 
         def x_copies(a):
-            t = const.tile([P, PACK * TOKENS], BF16, name="xg%d" % a, align_bytes=64)
+            t = work.tile([P, PACK * TOKENS], BF16, tag="stage", name="xg%d" % a, bufs=STAGE_BUFS, align_bytes=64)
             xg[a] = t
             tw = t[:].bitcast(F32).rearrange("p (g r u) -> p g r u", g=PASSES, u=2)
-            nc.vector.tensor_copy(out=tw[:, 0:2], in_=xbank[(a, 0)][:].rearrange("p g u r -> p g r u"))
+            first_copy = nc.scalar.copy if X_COPY_S else nc.vector.tensor_copy
+            first_copy(out=tw[:, 0:2], in_=xbank[(a, 0)][:].rearrange("p g u r -> p g r u"))
             nc.scalar.copy(out=tw[:, 2:4], in_=xbank[(a, 1)][:].rearrange("p g u r -> p g r u"))
 
         def x_quantize(a):
@@ -184,7 +210,8 @@ def tile_multiheadlatentattention_pb_kernel(tc, x, freq_cis, Wq, out):
                 copy_il(nc.scalar.copy, dst[:, :hg], src[:, :hg])
                 nc.gpsimd.tensor_scalar(out=dst[:, hg], in0=src[:, hg], scalar1=1.0, scalar2=0.0, op0=MULT, op1=ADD)
                 return
-            fs = SPLIT.get(pos, 0 if pos in V_UNITS else HALF)
+            sv = pos - IL_LEAD
+            fs = HALF if pos >= S_ONLY_FROM else FS_HEAD if pos < HEAD_UNITS else (FS_FREE, FS_ONE, FS_BOTH)[(1 if sv in rope_at else 0) + (1 if sv in sum_at else 0)]
             if fs > 0:
                 copy_il(nc.scalar.copy, dst[:, h0:h1, :fs, :], src[:, h0:h1, :fs, :], plain=(pos < 2))
             if fs < HALF:
@@ -219,7 +246,7 @@ def tile_multiheadlatentattention_pb_kernel(tc, x, freq_cis, Wq, out):
 
         def get_stage(c, a):
             if (c, a) not in stage:
-                stage[(c, a)] = work.tile([P, CHUNK], F32, tag="stage", name="st%d_%d" % (c, a), bufs=STAGE_BUFS)
+                stage[(c, a)] = work.tile([P, CHUNK], F32, tag="stage", name="st%d_%d" % (c, a), bufs=STAGE_BUFS, align_bytes=64)
             return stage[(c, a)][:].rearrange("p (h k f) -> p h k f", k=2, f=HALF)
 
         def finish(c, a):
@@ -284,5 +311,18 @@ def tile_multiheadlatentattention_pb_kernel(tc, x, freq_cis, Wq, out):
                 interleave(pos)
                 refill(pos)
 
+        if X_FIRST:
+            x_transposes(0)
+            x_transposes(1)
+            x_copies(0)
+            x_transposes(2)
+            x_copies(1)
+            x_quantize(0)
+            x_transposes(3)
+            x_copies(2)
+            x_quantize(1)
+            x_copies(3)
+            x_quantize(2)
+            x_quantize(3)
         for s in range(-IL_LEAD, n_steps):
             step(s)

@@ -30,6 +30,8 @@ UNITS = TILES * PASSES
 
 V_UNITS = (1, 4, 7, 10, 13, 15, 18, 21, 23, 26)
 KLAG = 0
+W0_CUTS = (0, 1024)
+FC_AFTER = 5
 X_FIRST = 1
 X_COPY_S = 0
 TAB_S = 0
@@ -56,7 +58,7 @@ SUM_LAG = 4
 UNSKEW_LAST = 1
 FAST_IL = 1
 X0 = 1
-TAB_STEP = 5
+TAB_STEP = 6
 W_FIRST = 3
 QW = 1
 
@@ -139,8 +141,8 @@ def tile_multiheadlatentattention_pb_kernel(tc, x, freq_cis, Wq, out):
         if X_FIRST:
             for a in range(TOK_TILES):
                 load_x(a)
-            load_w(0, (0, 256, 512, 1024))
-            for i in range(1, W_FIRST):
+            load_w(0, W0_CUTS)
+            for i in range(1, FC_AFTER):
                 load_w(i)
         else:
             load_w(0, (0, 256, 512, 1024))
@@ -149,7 +151,7 @@ def tile_multiheadlatentattention_pb_kernel(tc, x, freq_cis, Wq, out):
             for a in range(TOK_TILES):
                 load_x(a)
         nc.sync.dma_start(out=fc[:], in_=freq_cis.rearrange("(a p) i e -> p a (i e)", p=P))
-        for i in range(W_FIRST, RAW_BUFS):
+        for i in range(FC_AFTER if X_FIRST else W_FIRST, RAW_BUFS):
             load_w(i)
 
         def make_tables():
@@ -213,9 +215,9 @@ def tile_multiheadlatentattention_pb_kernel(tc, x, freq_cis, Wq, out):
             sv = pos - IL_LEAD
             fs = HALF if pos >= S_ONLY_FROM else FS_HEAD if pos < HEAD_UNITS else (FS_FREE, FS_ONE, FS_BOTH)[(1 if sv in rope_at else 0) + (1 if sv in sum_at else 0)]
             if fs > 0:
-                copy_il(nc.scalar.copy, dst[:, h0:h1, :fs, :], src[:, h0:h1, :fs, :], plain=(pos < 2))
+                copy_il(nc.scalar.copy, dst[:, h0:h1, :fs, :], src[:, h0:h1, :fs, :], plain=(pos < 2 and len(W0_CUTS) > 2))
             if fs < HALF:
-                copy_il(nc.vector.tensor_copy, dst[:, h0:h1, fs:, :], src[:, h0:h1, fs:, :], plain=(pos < 2))
+                copy_il(nc.vector.tensor_copy, dst[:, h0:h1, fs:, :], src[:, h0:h1, fs:, :], plain=(pos < 2 and len(W0_CUTS) > 2))
 
         def refill(pos):
             tile_i, g = order[pos]
@@ -303,9 +305,9 @@ def tile_multiheadlatentattention_pb_kernel(tc, x, freq_cis, Wq, out):
                 x_copies(a)
             pos = s + IL_LEAD
             if s == -IL_LEAD:
-                for h0, h1 in ((0, 1), (1, 2), (2, 4)):
-                    interleave(0, h0, h1)
-                    interleave(1, h0, h1)
+                for h0, h1 in zip(W0_CUTS[:-1], W0_CUTS[1:]):
+                    interleave(0, h0 // 256, h1 // 256)
+                    interleave(1, h0 // 256, h1 // 256)
                 refill(1)
             elif 2 <= pos < UNITS:
                 interleave(pos)

@@ -30,6 +30,7 @@ UNITS = TILES * PASSES
 
 V_UNITS = (1, 4, 7, 10, 13, 15, 18, 21, 23, 26)
 KLAG = 0
+MERGE = 2
 W0_CUTS = (0, 1024)
 FC_AFTER = 5
 X_FIRST = 1
@@ -51,8 +52,8 @@ RAW_BUFS = 10
 WG_BUFS = 6
 WC_BUFS = 10
 ACC_BUFS = 8
-PROD_BUFS = 5
-STAGE_BUFS = 12
+PROD_BUFS = 3
+STAGE_BUFS = 12 // MERGE
 IL_LEAD = 3
 SUM_LAG = 4
 UNSKEW_LAST = 1
@@ -122,7 +123,7 @@ def tile_multiheadlatentattention_pb_kernel(tc, x, freq_cis, Wq, out):
         ctx.enter_context(tc.manual_schedule())
         nc.scalar.copy(out=warm[:], in_=ident[:, 0:1])
 
-        raw, xraw, xg, xc, xs, xbank = {}, {}, {}, {}, {}, {}
+        raw, xraw, xg, xc, xs, xbank, xrawm, xgm = {}, {}, {}, {}, {}, {}, {}, {}
         wg, wc, ws, acc, prod, stage, done = {}, {}, {}, {}, {}, {}, {}
 
         def load_w(i, cuts=(0, CHUNK)):
@@ -134,9 +135,10 @@ def tile_multiheadlatentattention_pb_kernel(tc, x, freq_cis, Wq, out):
             raw[(c, g)] = t
 
         def load_x(a):
-            t = work.tile([P, K], BF16, tag="stage", name="xraw%d" % a, bufs=STAGE_BUFS, align_bytes=64)
-            nc.sync.dma_start(out=t[:], in_=x2[a * P:(a + 1) * P, :])
-            xraw[a] = t
+            if a % MERGE == 0:
+                xrawm[a // MERGE] = work.tile([P, MERGE, K], BF16, tag="stage", name="xraw%d" % a, bufs=STAGE_BUFS, align_bytes=64)
+            xraw[a] = xrawm[a // MERGE][:, a % MERGE]
+            nc.sync.dma_start(out=xraw[a], in_=x2[a * P:(a + 1) * P, :])
 
         if X_FIRST:
             for a in range(TOK_TILES):
@@ -169,7 +171,7 @@ def tile_multiheadlatentattention_pb_kernel(tc, x, freq_cis, Wq, out):
                 in1=sign[:].unsqueeze(1).unsqueeze(1).to_broadcast(shape), op=MULT)
 
         def x_transposes(a):
-            words = xraw[a][:].bitcast(F32)
+            words = xraw[a].bitcast(F32)
             for gp in range(2):
                 bank = psum.tile([P, 2, 2, P], F32, tag="acc", name="xb%d_%d" % (a, gp))
                 for g2 in range(2):
@@ -179,9 +181,10 @@ def tile_multiheadlatentattention_pb_kernel(tc, x, freq_cis, Wq, out):
                 xbank[(a, gp)] = bank
 
         def x_copies(a):
-            t = work.tile([P, PACK * TOKENS], BF16, tag="stage", name="xg%d" % a, bufs=STAGE_BUFS, align_bytes=64)
-            xg[a] = t
-            tw = t[:].bitcast(F32).rearrange("p (g r u) -> p g r u", g=PASSES, u=2)
+            if a % MERGE == 0:
+                xgm[a // MERGE] = work.tile([P, MERGE, PACK * TOKENS], BF16, tag="stage", name="xg%d" % a, bufs=STAGE_BUFS, align_bytes=64)
+            xg[a] = xgm[a // MERGE][:, a % MERGE]
+            tw = xg[a].bitcast(F32).rearrange("p (g r u) -> p g r u", g=PASSES, u=2)
             first_copy = nc.scalar.copy if X_COPY_S else nc.vector.tensor_copy
             first_copy(out=tw[:, 0:2], in_=xbank[(a, 0)][:].rearrange("p g u r -> p g r u"))
             nc.scalar.copy(out=tw[:, 2:4], in_=xbank[(a, 1)][:].rearrange("p g u r -> p g r u"))
@@ -189,7 +192,7 @@ def tile_multiheadlatentattention_pb_kernel(tc, x, freq_cis, Wq, out):
         def x_quantize(a):
             xc[a] = const.tile([P, TOKENS], U32, name="xc%d" % a, align_bytes=64)
             xs[a] = const.tile([P, TOKENS], U8, name="xs%d" % a, align_bytes=64)
-            nc.vector.quantize_mx(out=xc[a][:].bitcast(E5M2), scales=xs[a][:], in_=xg[a][:])
+            nc.vector.quantize_mx(out=xc[a][:].bitcast(E5M2), scales=xs[a][:], in_=xg[a])
 
         def copy_il(eng_copy, dst, src, plain=False):
             if plain:
@@ -247,35 +250,50 @@ def tile_multiheadlatentattention_pb_kernel(tc, x, freq_cis, Wq, out):
             )
 
         def get_stage(c, a):
-            if (c, a) not in stage:
-                stage[(c, a)] = work.tile([P, CHUNK], F32, tag="stage", name="st%d_%d" % (c, a), bufs=STAGE_BUFS, align_bytes=64)
-            return stage[(c, a)][:].rearrange("p (h k f) -> p h k f", k=2, f=HALF)
+            if (c, a // MERGE) not in stage:
+                stage[(c, a // MERGE)] = work.tile([P, MERGE, CHUNK], F32, tag="stage", name="st%d_%d" % (c, a), bufs=STAGE_BUFS, align_bytes=64)
+            return stage[(c, a // MERGE)][:, a % MERGE].rearrange("p (h k f) -> p h k f", k=2, f=HALF)
 
         def finish(c, a):
             done[(c, a)] = done.get((c, a), 0) + 1
             if done[(c, a)] == 2:
-                nc.sync.dma_start(out=out2[a * P:(a + 1) * P, c * CHUNK:(c + 1) * CHUNK], in_=stage[(c, a)][:])
+                nc.sync.dma_start(out=out2[a * P:(a + 1) * P, c * CHUNK:(c + 1) * CHUNK], in_=stage[(c, a // MERGE)][:, a % MERGE])
 
         def rope_products(tile_i, a):
-            t = work.tile([P, 2, N_TILE], F32, tag="prod", name="pr%d_%d" % (tile_i, a), bufs=PROD_BUFS)
-            prod[(tile_i, a)] = t
+            if a % MERGE == 0:
+                prod[(tile_i, a // MERGE)] = work.tile([P, MERGE, 2, N_TILE], F32, tag="prod", name="pr%d_%d" % (tile_i, a), bufs=PROD_BUFS)
+            t = prod[(tile_i, a // MERGE)][:, a % MERGE]
             shape = [P, 2, CHUNK_HEADS, HALF]
             nc.vector.tensor_tensor(
-                out=t[:].rearrange("p w (h f) -> p w h f", f=HALF),
+                out=t.rearrange("p w (h f) -> p w h f", f=HALF),
                 in0=acc[(tile_i, a)][:].rearrange("p (h f) -> p h f", f=HALF).unsqueeze(1).to_broadcast(shape),
                 in1=tab[:, a].unsqueeze(2).to_broadcast(shape),
                 op=MULT,
             )
 
         def rope_sum(tile_i, a):
-            t = prod[(tile_i, a)]
+            if tile_i == TILES - 2:
+                t = prod[(tile_i, a // MERGE)][:, a % MERGE]
+                nc.vector.tensor_tensor(
+                    out=get_stage(tile_i // 2, a)[:, :, 1, :].rearrange("p h (i e) -> p h i e", e=2),
+                    in0=t[:, 0].rearrange("p (h i e) -> p h i e", h=CHUNK_HEADS, e=2),
+                    in1=t[:, 1].rearrange("p (h i e) -> p h i e", h=CHUNK_HEADS, e=2)[:, :, :, ::-1],
+                    op=ADD,
+                )
+                finish(tile_i // 2, a)
+                return
+            if a % MERGE != MERGE - 1:
+                return
+            t = prod[(tile_i, a // MERGE)]
+            get_stage(tile_i // 2, a)
             nc.vector.tensor_tensor(
-                out=get_stage(tile_i // 2, a)[:, :, 1, :].rearrange("p h (i e) -> p h i e", e=2),
-                in0=t[:, 0].rearrange("p (h i e) -> p h i e", h=CHUNK_HEADS, e=2),
-                in1=t[:, 1].rearrange("p (h i e) -> p h i e", h=CHUNK_HEADS, e=2)[:, :, :, ::-1],
+                out=stage[(tile_i // 2, a // MERGE)][:].rearrange("p b (h k i e) -> p b h k i e", k=2, h=CHUNK_HEADS, e=2)[:, :, :, 1],
+                in0=t[:, :, 0].rearrange("p b (h i e) -> p b h i e", h=CHUNK_HEADS, e=2),
+                in1=t[:, :, 1].rearrange("p b (h i e) -> p b h i e", h=CHUNK_HEADS, e=2)[:, :, :, :, ::-1],
                 op=ADD,
             )
-            finish(tile_i // 2, a)
+            for b in range(MERGE):
+                finish(tile_i // 2, a - MERGE + 1 + b)
 
         def kept_copy(tile_i, a):
             nc.scalar.copy(

@@ -66,8 +66,8 @@ QW = 1
 
 def tile_multiheadlatentattention_pb_kernel(tc, x, freq_cis, Wq, out):
     nc = tc.nc
-    x2 = x.flatten_outer_dims()
-    out2 = out.rearrange("b t h d -> (b t) (h d)")
+    x2 = x.flatten_outer_dims().rearrange("(p a) k -> a p k", a=TOK_TILES)
+    out2 = out.rearrange("b (p a) h d -> a (b p) (h d)", a=TOK_TILES)
 
     order = []
     for c in range(ALT_CHUNKS):
@@ -138,7 +138,7 @@ def tile_multiheadlatentattention_pb_kernel(tc, x, freq_cis, Wq, out):
             if a % MERGE == 0:
                 xrawm[a // MERGE] = work.tile([P, MERGE, K], BF16, tag="stage", name="xraw%d" % a, bufs=STAGE_BUFS, align_bytes=64)
             xraw[a] = xrawm[a // MERGE][:, a % MERGE]
-            nc.sync.dma_start(out=xraw[a], in_=x2[a * P:(a + 1) * P, :])
+            nc.sync.dma_start(out=xraw[a], in_=x2[a])
 
         if X_FIRST:
             for a in range(TOK_TILES):
@@ -152,7 +152,7 @@ def tile_multiheadlatentattention_pb_kernel(tc, x, freq_cis, Wq, out):
                 load_w(i)
             for a in range(TOK_TILES):
                 load_x(a)
-        nc.sync.dma_start(out=fc[:], in_=freq_cis.rearrange("(a p) i e -> p a (i e)", p=P))
+        nc.sync.dma_start(out=fc[:], in_=freq_cis.rearrange("(p a) i e -> p a (i e)", p=P))
         for i in range(FC_AFTER if X_FIRST else W_FIRST, RAW_BUFS):
             load_w(i)
 
@@ -257,7 +257,7 @@ def tile_multiheadlatentattention_pb_kernel(tc, x, freq_cis, Wq, out):
         def finish(c, a):
             done[(c, a)] = done.get((c, a), 0) + 1
             if done[(c, a)] == 2:
-                nc.sync.dma_start(out=out2[a * P:(a + 1) * P, c * CHUNK:(c + 1) * CHUNK], in_=stage[(c, a // MERGE)][:, a % MERGE])
+                nc.sync.dma_start(out=out2[a][:, c * CHUNK:(c + 1) * CHUNK], in_=stage[(c, a // MERGE)][:, a % MERGE])
 
         def rope_products(tile_i, a):
             if a % MERGE == 0:

from contextlib import ExitStack

import concourse.mybir as mybir
from concourse.masks import make_identity

F32 = mybir.dt.float32
BF16 = mybir.dt.bfloat16
U32 = mybir.dt.uint32
U8 = mybir.dt.uint8
E4M3 = mybir.dt.float8_e4m3fn_x4
E5M2 = mybir.dt.float8_e5m2_x4
MULT = mybir.AluOpType.mult
ADD = mybir.AluOpType.add

TOKENS, K, FEATURES = 512, 2048, 4096
FLOPS = 2 * TOKENS * K * FEATURES

P = 128
PACK = 4
K_PASS = P * PACK
PASSES = K // K_PASS
TOK_TILES = TOKENS // P
N_TILE = 512
HALF = 128
CHUNK_HEADS = 4
CHUNK = CHUNK_HEADS * 2 * HALF
CHUNKS = FEATURES // CHUNK
TILES = 2 * CHUNKS
UNITS = TILES * PASSES

V_UNITS = (1, 4, 7, 10, 13, 15, 18, 21, 23, 26)
KLAG = 0
MERGE = 2
W0_CUTS = (0, 1024)
FC_AFTER = 5
X_FIRST = 1
X_COPY_S = 0
TAB_S = 0
HEAD_UNITS = 8
FS_HEAD = 64
KLAG_TILES = 2
S_ONLY_FROM = 28
FS_FREE = 80
FS_ONE = 80
FS_BOTH = 80
SEQ = (0, 1, 2, 3, 4, 5, 6, 7)
SUM_LAG_END = 1
END_TILES = 2
G_HELP = 1
ALT_CHUNKS = 2
RAW_BUFS = 10
WG_BUFS = 6
WC_BUFS = 10
ACC_BUFS = 8
PROD_BUFS = 3
STAGE_BUFS = 12 // MERGE
IL_LEAD = 3
SUM_LAG = 4
UNSKEW_LAST = 1
FAST_IL = 1
X0 = 1
TAB_STEP = 6
W_FIRST = 3
QW = 1


def tile_multiheadlatentattention_pb_kernel(tc, x, freq_cis, Wq, out):
    nc = tc.nc
    x2 = x.flatten_outer_dims().rearrange("(p a) k -> a p k", a=TOK_TILES)
    out2 = out.rearrange("b (p a) h d -> a (b p) (h d)", a=TOK_TILES)

    order = []
    for c in range(ALT_CHUNKS):
        for g in range(PASSES):
            order.extend([(2 * c, g), (2 * c + 1, g)])
    order.extend([(t, g) for t in SEQ[2 * ALT_CHUNKS:] for g in range(PASSES)])
    place = dict((unit, pos) for pos, unit in enumerate(order))
    made = dict((unit, QW * (pos // QW) + QW - 1) for pos, unit in enumerate(order))

    passes_at, rope_at, kept_at, sum_at = {}, {}, {}, {}
    x_tr_at = {} if X_FIRST else {X0: (0, 1), X0 + 1: (2, 3)}
    x_cp_at = {} if X_FIRST else {X0 + 1: (0, 1), X0 + 2: (2, 3)}
    x_q_at = {} if X_FIRST else {X0 + 2: (0, 1), X0 + 3: (2, 3)}
    freed = [-9] * 8 if X_FIRST else [X0 + 1] * 4 + [X0 + 2] * 4
    last_ep = {0: -9, 1: -9}
    last_sum = -9
    opened = -1 if X_FIRST else X0 + 3
    for n, tile_i in enumerate(SEQ):
        for a in range(TOK_TILES):
            skew = 0 if n >= TILES - UNSKEW_LAST else a
            st = max(n * PASSES + skew, freed[len(freed) - ACC_BUFS] + 1, opened)
            opened = st
            for g in range(PASSES):
                st = max(st + (1 if g else 0), made[(tile_i, g)])
                passes_at.setdefault(st, []).append((tile_i, a, g))
            kept = tile_i % 2
            ep = max(st + 1 + (KLAG if kept and n < KLAG_TILES else 0), last_ep[kept] + 1)
            if n == TILES - 1:
                ep = st + 1
            last_ep[kept] = ep
            freed.append(ep)
            (kept_at if kept else rope_at).setdefault(ep, []).append((tile_i, a))
            if not kept:
                last_sum = max(ep + (SUM_LAG if n < TILES - 1 - END_TILES else SUM_LAG_END), last_sum + 1)
                sum_at.setdefault(last_sum, []).append((tile_i, a))
    n_steps = max(max(kept_at), max(sum_at)) + 1

    with ExitStack() as ctx:
        const = ctx.enter_context(tc.tile_pool(name="const", bufs=1))
        rawp = ctx.enter_context(tc.tile_pool(name="rawp", bufs=RAW_BUFS))
        work = ctx.enter_context(tc.tile_pool(name="work", bufs=2))
        psum = ctx.enter_context(tc.psum_pool(name="psum", bufs=ACC_BUFS))

        ident = const.tile([P, P], F32, name="ident")
        make_identity(nc, ident[:])
        warm = const.tile([P, 1], F32, name="warm")
        sign = const.tile([P, 2], F32, name="sign")
        nc.gpsimd.memset(sign[:, 0:1], 1.0)
        nc.gpsimd.memset(sign[:, 1:2], -1.0)
        fc = const.tile([P, TOK_TILES, HALF], BF16, name="fc")
        tab = const.tile([P, TOK_TILES, 2, HALF], F32, name="tab")

        ctx.enter_context(tc.manual_schedule())
        nc.scalar.copy(out=warm[:], in_=ident[:, 0:1])

        raw, xraw, xg, xc, xs, xbank, xrawm, xgm = {}, {}, {}, {}, {}, {}, {}, {}
        wg, wc, ws, acc, prod, stage, done = {}, {}, {}, {}, {}, {}, {}

        def load_w(i, cuts=(0, CHUNK)):
            c, g = divmod(i, PASSES)
            t = rawp.tile([P, PACK, CHUNK], BF16, tag="raw", name="raw%d_%d" % (c, g))
            rows = Wq[g * K_PASS:(g + 1) * K_PASS, c * CHUNK:(c + 1) * CHUNK].rearrange("(p j) n -> p j n", j=PACK)
            for lo, hi in zip(cuts[:-1], cuts[1:]):
                nc.sync.dma_start(out=t[:, :, lo:hi], in_=rows[:, :, lo:hi])
            raw[(c, g)] = t

        def load_x(a):
            if a % MERGE == 0:
                xrawm[a // MERGE] = work.tile([P, MERGE, K], BF16, tag="stage", name="xraw%d" % a, bufs=STAGE_BUFS, align_bytes=64)
            xraw[a] = xrawm[a // MERGE][:, a % MERGE]
            nc.sync.dma_start(out=xraw[a], in_=x2[a])

        if X_FIRST:
            for a in range(TOK_TILES):
                load_x(a)
            load_w(0, W0_CUTS)
            for i in range(1, FC_AFTER):
                load_w(i)
        else:
            load_w(0, (0, 256, 512, 1024))
            for i in range(1, W_FIRST):
                load_w(i)
            for a in range(TOK_TILES):
                load_x(a)
        nc.sync.dma_start(out=fc[:], in_=freq_cis.rearrange("(p a) i e -> p a (i e)", p=P))
        for i in range(FC_AFTER if X_FIRST else W_FIRST, RAW_BUFS):
            load_w(i)

        def make_tables():
            fcv = fc[:].rearrange("p a (i e) -> p a i e", e=2)
            tabv = tab[:].rearrange("p a w (i e) -> p a w i e", e=2)
            shape = [P, TOK_TILES, HALF // 2, 2]
            if TAB_S:
                nc.scalar.copy(out=tabv[:, :, 0], in_=fcv[:, :, :, 0:1].to_broadcast(shape))
                nc.scalar.copy(out=tabv[:, :, 1, :, 0:1], in_=fcv[:, :, :, 1:2])
                nc.scalar.mul(out=tabv[:, :, 1, :, 1:2], in_=fcv[:, :, :, 1:2], mul=-1.0)
                return
            nc.vector.tensor_copy(out=tabv[:, :, 0], in_=fcv[:, :, :, 0:1].to_broadcast(shape))
            nc.vector.tensor_tensor(
                out=tabv[:, :, 1], in0=fcv[:, :, :, 1:2].to_broadcast(shape),
                in1=sign[:].unsqueeze(1).unsqueeze(1).to_broadcast(shape), op=MULT)

        def x_transposes(a):
            words = xraw[a].bitcast(F32)
            for gp in range(2):
                bank = psum.tile([P, 2, 2, P], F32, tag="acc", name="xb%d_%d" % (a, gp))
                for g2 in range(2):
                    g = 2 * gp + g2
                    for u in range(2):
                        nc.tensor.transpose(bank[:, g2, u, :], words[:, 256 * g + u:256 * (g + 1):2], ident[:])
                xbank[(a, gp)] = bank

        def x_copies(a):
            if a % MERGE == 0:
                xgm[a // MERGE] = work.tile([P, MERGE, PACK * TOKENS], BF16, tag="stage", name="xg%d" % a, bufs=STAGE_BUFS, align_bytes=64)
            xg[a] = xgm[a // MERGE][:, a % MERGE]
            tw = xg[a].bitcast(F32).rearrange("p (g r u) -> p g r u", g=PASSES, u=2)
            first_copy = nc.scalar.copy if X_COPY_S else nc.vector.tensor_copy
            first_copy(out=tw[:, 0:2], in_=xbank[(a, 0)][:].rearrange("p g u r -> p g r u"))
            nc.scalar.copy(out=tw[:, 2:4], in_=xbank[(a, 1)][:].rearrange("p g u r -> p g r u"))

        def x_quantize(a):
            xc[a] = const.tile([P, TOKENS], U32, name="xc%d" % a, align_bytes=64)
            xs[a] = const.tile([P, TOKENS], U8, name="xs%d" % a, align_bytes=64)
            nc.vector.quantize_mx(out=xc[a][:].bitcast(E5M2), scales=xs[a][:], in_=xg[a])

        def copy_il(eng_copy, dst, src, plain=False):
            if plain:
                eng_copy(out=dst, in_=src)
            elif FAST_IL:
                eng_copy(out=dst.rearrange("p h (b i) j -> p h b j i", i=4), in_=src.rearrange("p h (b i) j -> p h b j i", i=4))
            else:
                eng_copy(out=dst, in_=src)

        def interleave(pos, h0=0, h1=CHUNK_HEADS):
            tile_i, g = order[pos]
            c, kept = divmod(tile_i, 2)
            m, half = divmod(pos, QW)
            if m not in wg:
                wg[m] = work.tile([P, QW, PACK * N_TILE], BF16, tag="wg", name="wg%d" % m, bufs=WG_BUFS, align_bytes=64)
            src = raw[(c, g)][:].rearrange("p j (h k f) -> p k h f j", k=2, f=HALF)[:, 1 - kept]
            dst = wg[m][:, half].rearrange("p (h f j) -> p h f j", h=CHUNK_HEADS, j=PACK)
            if G_HELP and (pos - WG_BUFS - 1) in rope_at:
                hg = CHUNK_HEADS - 1
                copy_il(nc.scalar.copy, dst[:, :hg], src[:, :hg])
                nc.gpsimd.tensor_scalar(out=dst[:, hg], in0=src[:, hg], scalar1=1.0, scalar2=0.0, op0=MULT, op1=ADD)
                return
            sv = pos - IL_LEAD
            fs = HALF if pos >= S_ONLY_FROM else FS_HEAD if pos < HEAD_UNITS else (FS_FREE, FS_ONE, FS_BOTH)[(1 if sv in rope_at else 0) + (1 if sv in sum_at else 0)]
            if fs > 0:
                copy_il(nc.scalar.copy, dst[:, h0:h1, :fs, :], src[:, h0:h1, :fs, :], plain=(pos < 2 and len(W0_CUTS) > 2))
            if fs < HALF:
                copy_il(nc.vector.tensor_copy, dst[:, h0:h1, fs:, :], src[:, h0:h1, fs:, :], plain=(pos < 2 and len(W0_CUTS) > 2))

        def refill(pos):
            tile_i, g = order[pos]
            c, kept = divmod(tile_i, 2)
            i = c * PASSES + g + RAW_BUFS
            if kept and i < CHUNKS * PASSES:
                load_w(i)

        def quantize(m):
            wc[m] = work.tile([P, QW * N_TILE], U32, tag="wc", name="wc%d" % m, bufs=WC_BUFS, align_bytes=64)
            ws[m] = work.tile([P, QW * N_TILE], U8, tag="ws", name="ws%d" % m, bufs=WC_BUFS, align_bytes=64)
            nc.vector.quantize_mx(out=wc[m][:].bitcast(E4M3), scales=ws[m][:], in_=wg[m][:].rearrange("p q n -> p (q n)"))

        def mx_pass(tile_i, a, g):
            if g == 0:
                acc[(tile_i, a)] = psum.tile([P, N_TILE], F32, tag="acc", name="acc%d_%d" % (tile_i, a))
            m, half = divmod(place[(tile_i, g)], QW)
            cols = slice(half * N_TILE, (half + 1) * N_TILE)
            nc.tensor.matmul_mx(
                out=acc[(tile_i, a)][:],
                lhsT=xc[a][:, g * P:(g + 1) * P].bitcast(E5M2),
                lhsT_scale=xs[a][:, g * P:(g + 1) * P],
                rhs=wc[m][:, cols].bitcast(E4M3),
                rhs_scale=ws[m][:, cols],
                start=(g == 0),
                stop=(g == PASSES - 1),
            )

        def get_stage(c, a):
            if (c, a // MERGE) not in stage:
                stage[(c, a // MERGE)] = work.tile([P, MERGE, CHUNK], F32, tag="stage", name="st%d_%d" % (c, a), bufs=STAGE_BUFS, align_bytes=64)
            return stage[(c, a // MERGE)][:, a % MERGE].rearrange("p (h k f) -> p h k f", k=2, f=HALF)

        def finish(c, a):
            done[(c, a)] = done.get((c, a), 0) + 1
            if done[(c, a)] == 2:
                nc.sync.dma_start(out=out2[a][:, c * CHUNK:(c + 1) * CHUNK], in_=stage[(c, a // MERGE)][:, a % MERGE])

        def rope_products(tile_i, a):
            if a % MERGE == 0:
                prod[(tile_i, a // MERGE)] = work.tile([P, MERGE, 2, N_TILE], F32, tag="prod", name="pr%d_%d" % (tile_i, a), bufs=PROD_BUFS)
            t = prod[(tile_i, a // MERGE)][:, a % MERGE]
            shape = [P, 2, CHUNK_HEADS, HALF]
            nc.vector.tensor_tensor(
                out=t.rearrange("p w (h f) -> p w h f", f=HALF),
                in0=acc[(tile_i, a)][:].rearrange("p (h f) -> p h f", f=HALF).unsqueeze(1).to_broadcast(shape),
                in1=tab[:, a].unsqueeze(2).to_broadcast(shape),
                op=MULT,
            )

        def rope_sum(tile_i, a):
            if tile_i == TILES - 2:
                t = prod[(tile_i, a // MERGE)][:, a % MERGE]
                nc.vector.tensor_tensor(
                    out=get_stage(tile_i // 2, a)[:, :, 1, :].rearrange("p h (i e) -> p h i e", e=2),
                    in0=t[:, 0].rearrange("p (h i e) -> p h i e", h=CHUNK_HEADS, e=2),
                    in1=t[:, 1].rearrange("p (h i e) -> p h i e", h=CHUNK_HEADS, e=2)[:, :, :, ::-1],
                    op=ADD,
                )
                finish(tile_i // 2, a)
                return
            if a % MERGE != MERGE - 1:
                return
            t = prod[(tile_i, a // MERGE)]
            get_stage(tile_i // 2, a)
            nc.vector.tensor_tensor(
                out=stage[(tile_i // 2, a // MERGE)][:].rearrange("p b (h k i e) -> p b h k i e", k=2, h=CHUNK_HEADS, e=2)[:, :, :, 1],
                in0=t[:, :, 0].rearrange("p b (h i e) -> p b h i e", h=CHUNK_HEADS, e=2),
                in1=t[:, :, 1].rearrange("p b (h i e) -> p b h i e", h=CHUNK_HEADS, e=2)[:, :, :, :, ::-1],
                op=ADD,
            )
            for b in range(MERGE):
                finish(tile_i // 2, a - MERGE + 1 + b)

        def kept_copy(tile_i, a):
            nc.scalar.copy(
                out=get_stage(tile_i // 2, a)[:, :, 0, :],
                in_=acc[(tile_i, a)][:].rearrange("p (h f) -> p h f", f=HALF),
            )
            finish(tile_i // 2, a)

        def step(s):
            if 0 <= s + 1 < UNITS and (s + 1) % QW == QW - 1:
                quantize((s + 1) // QW)
            for a in x_q_at.get(s, ()):
                x_quantize(a)
            if s == TAB_STEP:
                make_tables()
            for a in x_tr_at.get(s, ()):
                x_transposes(a)
            for (tile_i, a, g) in passes_at.get(s, []):
                mx_pass(tile_i, a, g)
            for (tile_i, a) in rope_at.get(s, []):
                rope_products(tile_i, a)
            for (tile_i, a) in kept_at.get(s, []):
                kept_copy(tile_i, a)
            for (tile_i, a) in sum_at.get(s, []):
                rope_sum(tile_i, a)
            for a in x_cp_at.get(s, ()):
                x_copies(a)
            pos = s + IL_LEAD
            if s == -IL_LEAD:
                for h0, h1 in zip(W0_CUTS[:-1], W0_CUTS[1:]):
                    interleave(0, h0 // 256, h1 // 256)
                    interleave(1, h0 // 256, h1 // 256)
                refill(1)
            elif 2 <= pos < UNITS:
                interleave(pos)
                refill(pos)

        if X_FIRST:
            x_transposes(0)
            x_transposes(1)
            x_copies(0)
            x_transposes(2)
            x_copies(1)
            x_quantize(0)
            x_transposes(3)
            x_copies(2)
            x_quantize(1)
            x_copies(3)
            x_quantize(2)
            x_quantize(3)
        for s in range(-IL_LEAD, n_steps):
            step(s)
